import numpy as np
import ml_dtypes


def mxq(x, axis, fmt="e4m3"):
    dtype, down = {"e4m3": (ml_dtypes.float8_e4m3fn, 7), "e5m2": (ml_dtypes.float8_e5m2, 14)}[fmt]
    v = np.moveaxis(np.asarray(x, np.float32).astype(ml_dtypes.bfloat16).astype(np.float64), axis, -1)
    blocks = v.reshape(v.shape[:-1] + (-1, 32))
    amax = np.abs(blocks).max(-1, keepdims=True)
    byte = np.maximum(np.where(amax > 0, np.frexp(amax)[1] - 1 + 127, 0) - down, 1)
    scale = np.exp2(byte - 127.0)
    codes = (blocks / scale).astype(np.float32).astype(dtype).astype(np.float64)
    return np.moveaxis((codes * scale).reshape(v.shape), -1, axis)


WIDE = False


def mx_kscale(k):
    if not WIDE:
        return np.ones(k)
    levels = np.array([10, -10, 5, -5, 0])
    a = np.random.permutation(np.resize(levels, k // 512 * 4)).reshape(k // 512, 4)
    idx = np.arange(k)
    return np.exp2(a[idx // 512, idx % 128 // 32])


BF16 = ml_dtypes.bfloat16


def bf(x):
    return np.asarray(x, np.float32).astype(BF16)


def f64(x):
    return np.asarray(x).astype(np.float64)


B, S = 2, 128
FEATURES = 1024
HIDDEN = 4096


def gelu_tanh(v):
    return 0.5 * v * (1.0 + np.tanh(np.sqrt(2.0 / np.pi) * (v + 0.044715 * v**3)))


def setup_inputs():
    s, t = mx_kscale(FEATURES), mx_kscale(HIDDEN)
    x = np.random.standard_normal((B, S, FEATURES)) * s
    wg = np.random.standard_normal((2, FEATURES, HIDDEN)) * 0.03 / s[None, :, None]
    wg[1] = wg[1] * t
    wl = np.random.standard_normal((HIDDEN, FEATURES)) * 0.03 / t[:, None]
    return {"x": bf(x), "w_gating": bf(wg), "w_linear": bf(wl)}


def reference(x, w_gating, w_linear):
    xq = mxq(f64(x), 2, "e4m3")
    wg = f64(w_gating)
    ff_gate = xq @ mxq(wg[0], 0, "e4m3")
    gate_value = gelu_tanh(ff_gate)
    ff1 = xq @ mxq(wg[1], 0, "e4m3")
    activations = gate_value * ff1
    outputs = mxq(activations, 2, "e4m3") @ mxq(f64(w_linear), 0, "e4m3")
    return outputs

@@ -1,0 +1,258 @@
+from contextlib import ExitStack
+
+import concourse.mybir as mybir
+from concourse.masks import make_identity
+
+F32 = mybir.dt.float32
+BF16 = mybir.dt.bfloat16
+U32 = mybir.dt.uint32
+U8 = mybir.dt.uint8
+FP8X4 = mybir.dt.float8_e4m3fn_x4
+GELU = mybir.ActivationFunctionType.Gelu_apprx_tanh
+MULT = mybir.AluOpType.mult
+
+P = 128
+PACK = 4
+K_PASS = P * PACK
+TOKENS = 256
+FEATURES = 1024
+HIDDEN = 4096
+UNIT = 1024
+FLOPS = 2 * TOKENS * FEATURES * HIDDEN * 3
+
+RAW_BUFS = 8
+GRP_BUFS = 3
+CODE_BUFS = 10
+X_AFTER = 0
+X_SLOT = 2
+LAG = 5
+CUT_PLAIN = 496
+CUT_BUSY = 464
+
+
+def tile_feedforwardsimple_kernel(tc, x, w_gating, w_linear, out):
+    nc = tc.nc
+    n_ranges = HIDDEN // UNIT
+    units = [("g", r, i, c) for r in range(n_ranges) for i in range(2) for c in range(2)]
+    n_gate_units = len(units)
+    n_blocks = HIDDEN // K_PASS
+    units = units + [("l", g, 0, 0) for g in range(n_blocks)]
+    n_units = len(units)
+    n_epi = 2 * n_blocks
+
+    gelu_slot = [e + LAG for e in range(n_epi)]
+    mul_slot = [s + 1 for s in gelu_slot]
+
+    def pair_of(e):
+        return e % 4 if e < n_epi - 4 else e % 2
+
+    def prev_user(e):
+        users = [f for f in range(e) if pair_of(f) == pair_of(e)]
+        return users[-1] if users else None
+
+    mm1_slot = []
+    for e in range(n_epi):
+        s = max(4 * (e // 4) + 3, X_SLOT + 1)
+        if prev_user(e) is not None:
+            s = max(s, mul_slot[prev_user(e)])
+        mm1_slot.append(s)
+    qh_slot = [mul_slot[2 * g + 1] + 1 for g in range(n_blocks)]
+    mm2_slot = [max(n_gate_units + g, qh_slot[g], mul_slot[n_epi - 5]) for g in range(n_blocks)]
+
+    with ExitStack() as ctx:
+        keep = ctx.enter_context(tc.tile_pool(name="keep", bufs=1))
+        rawp = ctx.enter_context(tc.tile_pool(name="rawp", bufs=RAW_BUFS))
+        grpp = ctx.enter_context(tc.tile_pool(name="grpp", bufs=GRP_BUFS))
+        codp = ctx.enter_context(tc.tile_pool(name="codp", bufs=CODE_BUFS))
+        gelp = ctx.enter_context(tc.tile_pool(name="gelp", bufs=3))
+        ostp = ctx.enter_context(tc.tile_pool(name="ostp", bufs=4))
+        psum = ctx.enter_context(tc.psum_pool(name="psum", bufs=1))
+        ctx.enter_context(tc.manual_schedule())
+
+        raw = {}
+        grp = {}
+        codes = {}
+        scales = {}
+        gate_ps = {}
+        lin_ps = {}
+        gel = {}
+        out_ps = {}
+
+        ident = keep.tile([P, P], F32, name="ident")
+        warm_in = keep.tile([P, 1], F32, name="warm_in")
+        warm_out = keep.tile([P, 1], F32, name="warm_out")
+        x_sb = keep.tile([P, 2 * FEATURES], BF16, name="x_sb")
+        xg = keep.tile([P, 2 * TOKENS * PACK], BF16, name="xg", align_bytes=64)
+        xcodes = keep.tile([P, 2 * TOKENS], U32, name="xcodes", align_bytes=64)
+        xscales = keep.tile([P, 2 * TOKENS], U8, name="xscales", align_bytes=64)
+        hg = keep.tile([P, n_blocks, TOKENS, PACK], BF16, name="hg", align_bytes=64)
+        hcodes = keep.tile([P, n_blocks * TOKENS], U32, name="hcodes", align_bytes=64)
+        hscales = keep.tile([P, n_blocks * TOKENS], U8, name="hscales", align_bytes=64)
+
+        def load(u):
+            kind, a, i, c = units[u]
+            raw[u] = rawp.tile([P, PACK, UNIT], BF16, name="raw", tag="raw")
+            if kind == "g":
+                src = w_gating[i, c * K_PASS : (c + 1) * K_PASS, a * UNIT : (a + 1) * UNIT].rearrange(
+                    "(p j) w -> p j w", j=PACK
+                )
+            else:
+                src = w_linear[a * K_PASS : (a + 1) * K_PASS, :].rearrange("(t p) n -> p t n", p=P)
+            nc.sync.dma_start(out=raw[u][:], in_=src)
+
+        def regroup(u, lo, hi, cut):
+            if u not in grp:
+                grp[u] = grpp.tile([P, UNIT, PACK], BF16, name="grp", tag="grp", align_bytes=64)
+            dst = grp[u][:, lo:cut, :].rearrange("p (c i) t -> p c t i", i=4)
+            src = raw[u][:, :, lo:cut].rearrange("p t (c i) -> p c t i", i=4)
+            nc.vector.tensor_copy(out=dst, in_=src)
+            dst = grp[u][:, cut:hi, :].rearrange("p (c i) t -> p c t i", i=4)
+            src = raw[u][:, :, cut:hi].rearrange("p t (c i) -> p c t i", i=4)
+            nc.scalar.copy(out=dst, in_=src)
+
+        def quantise(u, lo, hi):
+            if u not in codes:
+                codes[u] = codp.tile([P, UNIT], U32, name="codes", tag="codes", align_bytes=64)
+                scales[u] = codp.tile([P, UNIT], U8, name="scales", tag="scales", align_bytes=64)
+            nc.vector.quantize_mx(
+                out=codes[u][:, lo:hi].bitcast(FP8X4),
+                scales=scales[u][:, lo:hi],
+                in_=grp[u][:, lo:hi, :].rearrange("p w j -> p (w j)"),
+            )
+
+        def stage1(e):
+            g, a = e // 2, e % 2
+            r, off = g // 2, (g % 2) * K_PASS
+            q = pair_of(e)
+            gate_ps[e] = psum.tile([P, PACK, P], F32, name="gate_ps", tag="ps%d" % (2 * q))
+            lin_ps[e] = psum.tile([P, PACK, P], F32, name="lin_ps", tag="ps%d" % (2 * q + 1))
+            for i, bank in ((0, gate_ps[e]), (1, lin_ps[e])):
+                for t in range(PACK):
+                    for c in range(2):
+                        u = 4 * r + 2 * i + c
+                        cols = slice(off + t * P, off + (t + 1) * P)
+                        toks = slice(c * TOKENS + a * P, c * TOKENS + (a + 1) * P)
+                        nc.tensor.matmul_mx(
+                            out=bank[:, t, :],
+                            lhsT=codes[u][:, cols].bitcast(FP8X4),
+                            lhsT_scale=scales[u][:, cols],
+                            rhs=xcodes[:, toks].bitcast(FP8X4),
+                            rhs_scale=xscales[:, toks],
+                            start=(c == 0),
+                            stop=(c == 1),
+                        )
+
+        def gelu(e):
+            gel[e] = gelp.tile([P, P, PACK], F32, name="gel", tag="gel")
+            nc.scalar.activation(out=gel[e][:], in_=gate_ps[e][:].rearrange("p t k -> p k t"), func=GELU)
+
+        def gated(e):
+            g, a = e // 2, e % 2
+            nc.vector.tensor_tensor(
+                out=hg[:, g, a * P : (a + 1) * P, :],
+                in0=gel[e][:],
+                in1=lin_ps[e][:].rearrange("p t k -> p k t"),
+                op=MULT,
+            )
+
+        def quantise_h(g):
+            cols = slice(g * TOKENS, (g + 1) * TOKENS)
+            nc.vector.quantize_mx(
+                out=hcodes[:, cols].bitcast(FP8X4),
+                scales=hscales[:, cols],
+                in_=hg[:, g, :, :].rearrange("p k t -> p (k t)"),
+            )
+
+        def stage2(g, halves):
+            u = n_gate_units + g
+            for nh in halves:
+                for a in range(2):
+                    if (a, nh) not in out_ps:
+                        out_ps[(a, nh)] = psum.tile([P, 512], F32, name="out_ps", tag="ps%d" % (4 + 2 * a + nh))
+                    toks = slice(g * TOKENS + a * P, g * TOKENS + (a + 1) * P)
+                    cols = slice(nh * 512, (nh + 1) * 512)
+                    nc.tensor.matmul_mx(
+                        out=out_ps[(a, nh)][:],
+                        lhsT=hcodes[:, toks].bitcast(FP8X4),
+                        lhsT_scale=hscales[:, toks],
+                        rhs=codes[u][:, cols].bitcast(FP8X4),
+                        rhs_scale=scales[u][:, cols],
+                        start=(g == 0),
+                        stop=(g == n_blocks - 1),
+                    )
+
+        def store(a, nh, on_vector):
+            res = ostp.tile([P, 512], F32, name="res", tag="res")
+            if on_vector:
+                nc.vector.tensor_copy(out=res[:], in_=out_ps[(a, nh)][:])
+            else:
+                nc.scalar.copy(out=res[:], in_=out_ps[(a, nh)][:])
+            nc.sync.dma_start(out=out[a, :, nh * 512 : (nh + 1) * 512], in_=res[:])
+
+        def cut_of(u):
+            return CUT_BUSY if gelu_slot[0] <= u - 1 <= mul_slot[-1] else CUT_PLAIN
+
+        nc.vector.memset(warm_in[:], 0.0)
+        nc.scalar.activation(out=warm_out[:], in_=warm_in[:], func=GELU)
+        make_identity(nc, ident[:])
+        for u in range(RAW_BUFS):
+            load(u)
+            if u == X_AFTER:
+                nc.sync.dma_start(
+                    out=x_sb[:].rearrange("p (a k) -> p a k", a=2), in_=x.rearrange("a p k -> p a k")
+                )
+        xw = x_sb[:].bitcast(F32).rearrange("p (a c w u) -> p a c u w", a=2, c=2, w=P, u=2)
+        xgw = xg[:].bitcast(F32).rearrange("p (c k u) -> p c k u", c=2, k=TOKENS, u=2)
+        xt = {}
+        for c in range(2):
+            xt[c] = psum.tile([P, 2, TOKENS], F32, name="xt", tag="ps%d" % c)
+            for u in range(2):
+                for a in range(2):
+                    nc.tensor.transpose(xt[c][:, u, a * P : (a + 1) * P], xw[:, a, c, u, :], ident[:])
+        regroup(0, 0, UNIT, cut_of(0))
+        load(RAW_BUFS)
+
+        last = n_units - 1
+        for s in range(n_units):
+            nxt = s + 1
+            if nxt < last:
+                regroup(nxt, 0, UNIT, cut_of(nxt))
+            elif nxt == last:
+                regroup(nxt, 0, UNIT // 2, cut_of(nxt) // 2)
+                regroup(nxt, UNIT // 2, UNIT, UNIT // 2 + cut_of(nxt) // 2)
+            if nxt + RAW_BUFS < n_units:
+                load(nxt + RAW_BUFS)
+            if s < last:
+                quantise(s, 0, UNIT)
+            else:
+                quantise(s, 0, UNIT // 2)
+            if s == X_SLOT:
+                nc.vector.tensor_copy(out=xgw[:, 0], in_=xt[0][:].rearrange("p u k -> p k u"))
+                nc.scalar.copy(out=xgw[:, 1], in_=xt[1][:].rearrange("p u k -> p k u"))
+            if s == X_SLOT + 1:
+                nc.vector.quantize_mx(out=xcodes[:].bitcast(FP8X4), scales=xscales[:], in_=xg[:])
+            for e in range(n_epi):
+                if gelu_slot[e] == s:
+                    gelu(e)
+            for e in range(n_epi):
+                if mul_slot[e] == s:
+                    gated(e)
+            for g in range(n_blocks):
+                if qh_slot[g] == s:
+                    quantise_h(g)
+            for e in range(n_epi):
+                if mm1_slot[e] == s:
+                    stage1(e)
+            for g in range(n_blocks):
+                if mm2_slot[g] == s:
+                    if g < n_blocks - 1:
+                        stage2(g, (0, 1))
+                    else:
+                        stage2(g, (0,))
+
+        quantise(last, UNIT // 2, UNIT)
+        stage2(n_blocks - 1, (1,))
+        store(0, 0, False)
+        store(1, 0, False)
+        store(0, 1, True)
+        store(1, 1, False)

@@ -26,8 +26,8 @@ CODE_BUFS = 10
 X_AFTER = 0
 X_SLOT = 2
 LAG = 5
-CUT_PLAIN = 496
-CUT_BUSY = 464
+CUT_PLAIN = 528
+CUT_BUSY = 496
 
 
 def tile_feedforwardsimple_kernel(tc, x, w_gating, w_linear, out):

@@ -26,8 +26,8 @@ CODE_BUFS = 10
 X_AFTER = 0
 X_SLOT = 2
 LAG = 5
-CUT_PLAIN = 528
-CUT_BUSY = 496
+CUT_PLAIN = 496
+CUT_BUSY = 464
 
 
 def tile_feedforwardsimple_kernel(tc, x, w_gating, w_linear, out):
@@ -67,7 +67,6 @@ def tile_feedforwardsimple_kernel(tc, x, w_gating, w_linear, out):
         gelp = ctx.enter_context(tc.tile_pool(name="gelp", bufs=3))
         ostp = ctx.enter_context(tc.tile_pool(name="ostp", bufs=4))
         psum = ctx.enter_context(tc.psum_pool(name="psum", bufs=1))
-        ctx.enter_context(tc.manual_schedule())
 
         raw = {}
         grp = {}

@@ -20,14 +20,14 @@ HIDDEN = 4096
 UNIT = 1024
 FLOPS = 2 * TOKENS * FEATURES * HIDDEN * 3
 
-RAW_BUFS = 8
-GRP_BUFS = 3
+RAW_BUFS = 10
+GRP_BUFS = 4
 CODE_BUFS = 10
 X_AFTER = 0
 X_SLOT = 2
 LAG = 5
-CUT_PLAIN = 496
-CUT_BUSY = 464
+CUT_PLAIN = 504
+CUT_BUSY = 472
 
 
 def tile_feedforwardsimple_kernel(tc, x, w_gating, w_linear, out):

@@ -20,14 +20,18 @@ HIDDEN = 4096
 UNIT = 1024
 FLOPS = 2 * TOKENS * FEATURES * HIDDEN * 3
 
-RAW_BUFS = 10
-GRP_BUFS = 4
+RAW_BUFS = 8
+GRP_BUFS = 3
 CODE_BUFS = 10
 X_AFTER = 0
 X_SLOT = 2
 LAG = 5
-CUT_PLAIN = 504
-CUT_BUSY = 472
+CUT_PLAIN = 496
+CUT_BUSY = 464
+CUT_HELPED = 288
+HELPED = tuple(range(9, 18))
+GROUP = 256
+GROUPS = 2
 
 
 def tile_feedforwardsimple_kernel(tc, x, w_gating, w_linear, out):
@@ -44,7 +48,7 @@ def tile_feedforwardsimple_kernel(tc, x, w_gating, w_linear, out):
     mul_slot = [s + 1 for s in gelu_slot]
 
     def pair_of(e):
-        return e % 4 if e < n_epi - 4 else e % 2
+        return e % 3 if e < n_epi - 4 else e % 2
 
     def prev_user(e):
         users = [f for f in range(e) if pair_of(f) == pair_of(e)]
@@ -67,6 +71,7 @@ def tile_feedforwardsimple_kernel(tc, x, w_gating, w_linear, out):
         gelp = ctx.enter_context(tc.tile_pool(name="gelp", bufs=3))
         ostp = ctx.enter_context(tc.tile_pool(name="ostp", bufs=4))
         psum = ctx.enter_context(tc.psum_pool(name="psum", bufs=1))
+        ctx.enter_context(tc.manual_schedule())
 
         raw = {}
         grp = {}
@@ -78,6 +83,7 @@ def tile_feedforwardsimple_kernel(tc, x, w_gating, w_linear, out):
         out_ps = {}
 
         ident = keep.tile([P, P], F32, name="ident")
+        ident_bf = keep.tile([P, P], BF16, name="ident_bf")
         warm_in = keep.tile([P, 1], F32, name="warm_in")
         warm_out = keep.tile([P, 1], F32, name="warm_out")
         x_sb = keep.tile([P, 2 * FEATURES], BF16, name="x_sb")
@@ -105,9 +111,26 @@ def tile_feedforwardsimple_kernel(tc, x, w_gating, w_linear, out):
             dst = grp[u][:, lo:cut, :].rearrange("p (c i) t -> p c t i", i=4)
             src = raw[u][:, :, lo:cut].rearrange("p t (c i) -> p c t i", i=4)
             nc.vector.tensor_copy(out=dst, in_=src)
-            dst = grp[u][:, cut:hi, :].rearrange("p (c i) t -> p c t i", i=4)
-            src = raw[u][:, :, cut:hi].rearrange("p t (c i) -> p c t i", i=4)
+            top = hi - GROUPS * GROUP if u in HELPED else hi
+            dst = grp[u][:, cut:top, :].rearrange("p (c i) t -> p c t i", i=4)
+            src = raw[u][:, :, cut:top].rearrange("p t (c i) -> p c t i", i=4)
             nc.scalar.copy(out=dst, in_=src)
+            woven = {}
+            for k in range((hi - top) // GROUP):
+                cols = slice(top + k * GROUP, top + (k + 1) * GROUP)
+                woven[k] = psum.tile([P, GROUP, PACK], BF16, name="woven", tag="ps%d" % (6 + k))
+                words = woven[k][:].rearrange("p c t -> p (c t)").bitcast(F32).rearrange("p (c h) -> p c h", h=2)
+                for h in range(2):
+                    nc.tensor.matmul(
+                        out=words[:, :, h], lhsT=ident_bf[:], rhs=raw[u][:, 2 * h + 1, cols], start=True, stop=True
+                    )
+                for h in range(2):
+                    nc.tensor.matmul(
+                        out=woven[k][:, :, 2 * h], lhsT=ident_bf[:], rhs=raw[u][:, 2 * h, cols], start=True, stop=True
+                    )
+            for k in range((hi - top) // GROUP):
+                cols = slice(top + k * GROUP, top + (k + 1) * GROUP)
+                nc.scalar.copy(out=grp[u][:, cols, :], in_=woven[k][:])
 
         def quantise(u, lo, hi):
             if u not in codes:
@@ -189,11 +212,14 @@ def tile_feedforwardsimple_kernel(tc, x, w_gating, w_linear, out):
             nc.sync.dma_start(out=out[a, :, nh * 512 : (nh + 1) * 512], in_=res[:])
 
         def cut_of(u):
+            if u in HELPED:
+                return CUT_HELPED
             return CUT_BUSY if gelu_slot[0] <= u - 1 <= mul_slot[-1] else CUT_PLAIN
 
         nc.vector.memset(warm_in[:], 0.0)
         nc.scalar.activation(out=warm_out[:], in_=warm_in[:], func=GELU)
         make_identity(nc, ident[:])
+        make_identity(nc, ident_bf[:])
         for u in range(RAW_BUFS):
             load(u)
             if u == X_AFTER:

@@ -28,7 +28,7 @@ X_SLOT = 2
 LAG = 5
 CUT_PLAIN = 496
 CUT_BUSY = 464
-CUT_HELPED = 288
+CUT_HELPED = 352
 HELPED = tuple(range(9, 18))
 GROUP = 256
 GROUPS = 2
@@ -48,7 +48,7 @@ def tile_feedforwardsimple_kernel(tc, x, w_gating, w_linear, out):
     mul_slot = [s + 1 for s in gelu_slot]
 
     def pair_of(e):
-        return e % 3 if e < n_epi - 4 else e % 2
+        return e % 2
 
     def prev_user(e):
         users = [f for f in range(e) if pair_of(f) == pair_of(e)]
@@ -61,7 +61,7 @@ def tile_feedforwardsimple_kernel(tc, x, w_gating, w_linear, out):
             s = max(s, mul_slot[prev_user(e)])
         mm1_slot.append(s)
     qh_slot = [mul_slot[2 * g + 1] + 1 for g in range(n_blocks)]
-    mm2_slot = [max(n_gate_units + g, qh_slot[g], mul_slot[n_epi - 5]) for g in range(n_blocks)]
+    mm2_slot = [max(n_gate_units + g, qh_slot[g]) for g in range(n_blocks)]
 
     with ExitStack() as ctx:
         keep = ctx.enter_context(tc.tile_pool(name="keep", bufs=1))
@@ -81,6 +81,7 @@ def tile_feedforwardsimple_kernel(tc, x, w_gating, w_linear, out):
         lin_ps = {}
         gel = {}
         out_ps = {}
+        woven = {}
 
         ident = keep.tile([P, P], F32, name="ident")
         ident_bf = keep.tile([P, P], BF16, name="ident_bf")
@@ -115,22 +116,25 @@ def tile_feedforwardsimple_kernel(tc, x, w_gating, w_linear, out):
             dst = grp[u][:, cut:top, :].rearrange("p (c i) t -> p c t i", i=4)
             src = raw[u][:, :, cut:top].rearrange("p t (c i) -> p c t i", i=4)
             nc.scalar.copy(out=dst, in_=src)
-            woven = {}
             for k in range((hi - top) // GROUP):
                 cols = slice(top + k * GROUP, top + (k + 1) * GROUP)
-                woven[k] = psum.tile([P, GROUP, PACK], BF16, name="woven", tag="ps%d" % (6 + k))
-                words = woven[k][:].rearrange("p c t -> p (c t)").bitcast(F32).rearrange("p (c h) -> p c h", h=2)
+                nc.scalar.copy(out=grp[u][:, cols, :], in_=woven[(u, k)][:])
+
+        def weave(u):
+            top = UNIT - GROUPS * GROUP
+            for k in range(GROUPS):
+                cols = slice(top + k * GROUP, top + (k + 1) * GROUP)
+                bank = psum.tile([P, GROUP, PACK], BF16, name="woven", tag="ps%d" % (4 + 2 * (u % 2) + k))
+                woven[(u, k)] = bank
+                words = bank[:].rearrange("p c t -> p (c t)").bitcast(F32).rearrange("p (c h) -> p c h", h=2)
                 for h in range(2):
                     nc.tensor.matmul(
                         out=words[:, :, h], lhsT=ident_bf[:], rhs=raw[u][:, 2 * h + 1, cols], start=True, stop=True
                     )
                 for h in range(2):
                     nc.tensor.matmul(
-                        out=woven[k][:, :, 2 * h], lhsT=ident_bf[:], rhs=raw[u][:, 2 * h, cols], start=True, stop=True
+                        out=bank[:, :, 2 * h], lhsT=ident_bf[:], rhs=raw[u][:, 2 * h, cols], start=True, stop=True
                     )
-            for k in range((hi - top) // GROUP):
-                cols = slice(top + k * GROUP, top + (k + 1) * GROUP)
-                nc.scalar.copy(out=grp[u][:, cols, :], in_=woven[k][:])
 
         def quantise(u, lo, hi):
             if u not in codes:
@@ -265,6 +269,8 @@ def tile_feedforwardsimple_kernel(tc, x, w_gating, w_linear, out):
             for g in range(n_blocks):
                 if qh_slot[g] == s:
                     quantise_h(g)
+            if s + 2 in HELPED:
+                weave(s + 2)
             for e in range(n_epi):
                 if mm1_slot[e] == s:
                     stage1(e)

from contextlib import ExitStack

import concourse.mybir as mybir
from concourse.masks import make_identity

F32 = mybir.dt.float32
BF16 = mybir.dt.bfloat16
U32 = mybir.dt.uint32
U8 = mybir.dt.uint8
FP8X4 = mybir.dt.float8_e4m3fn_x4
GELU = mybir.ActivationFunctionType.Gelu_apprx_tanh
MULT = mybir.AluOpType.mult

P = 128
PACK = 4
K_PASS = P * PACK
TOKENS = 256
FEATURES = 1024
HIDDEN = 4096
UNIT = 1024
FLOPS = 2 * TOKENS * FEATURES * HIDDEN * 3

RAW_BUFS = 8
GRP_BUFS = 3
CODE_BUFS = 10
X_AFTER = 0
X_SLOT = 2
LAG = 5
CUT_PLAIN = 496
CUT_BUSY = 464
CUT_HELPED = 352
HELPED = tuple(range(9, 18))
GROUP = 256
GROUPS = 2


def tile_feedforwardsimple_kernel(tc, x, w_gating, w_linear, out):
    nc = tc.nc
    n_ranges = HIDDEN // UNIT
    units = [("g", r, i, c) for r in range(n_ranges) for i in range(2) for c in range(2)]
    n_gate_units = len(units)
    n_blocks = HIDDEN // K_PASS
    units = units + [("l", g, 0, 0) for g in range(n_blocks)]
    n_units = len(units)
    n_epi = 2 * n_blocks

    gelu_slot = [e + LAG for e in range(n_epi)]
    mul_slot = [s + 1 for s in gelu_slot]

    def pair_of(e):
        return e % 2

    def prev_user(e):
        users = [f for f in range(e) if pair_of(f) == pair_of(e)]
        return users[-1] if users else None

    mm1_slot = []
    for e in range(n_epi):
        s = max(4 * (e // 4) + 3, X_SLOT + 1)
        if prev_user(e) is not None:
            s = max(s, mul_slot[prev_user(e)])
        mm1_slot.append(s)
    qh_slot = [mul_slot[2 * g + 1] + 1 for g in range(n_blocks)]
    mm2_slot = [max(n_gate_units + g, qh_slot[g]) for g in range(n_blocks)]

    with ExitStack() as ctx:
        keep = ctx.enter_context(tc.tile_pool(name="keep", bufs=1))
        rawp = ctx.enter_context(tc.tile_pool(name="rawp", bufs=RAW_BUFS))
        grpp = ctx.enter_context(tc.tile_pool(name="grpp", bufs=GRP_BUFS))
        codp = ctx.enter_context(tc.tile_pool(name="codp", bufs=CODE_BUFS))
        gelp = ctx.enter_context(tc.tile_pool(name="gelp", bufs=3))
        ostp = ctx.enter_context(tc.tile_pool(name="ostp", bufs=4))
        psum = ctx.enter_context(tc.psum_pool(name="psum", bufs=1))
        ctx.enter_context(tc.manual_schedule())

        raw = {}
        grp = {}
        codes = {}
        scales = {}
        gate_ps = {}
        lin_ps = {}
        gel = {}
        out_ps = {}
        woven = {}

        ident = keep.tile([P, P], F32, name="ident")
        ident_bf = keep.tile([P, P], BF16, name="ident_bf")
        warm_in = keep.tile([P, 1], F32, name="warm_in")
        warm_out = keep.tile([P, 1], F32, name="warm_out")
        x_sb = keep.tile([P, 2 * FEATURES], BF16, name="x_sb")
        xg = keep.tile([P, 2 * TOKENS * PACK], BF16, name="xg", align_bytes=64)
        xcodes = keep.tile([P, 2 * TOKENS], U32, name="xcodes", align_bytes=64)
        xscales = keep.tile([P, 2 * TOKENS], U8, name="xscales", align_bytes=64)
        hg = keep.tile([P, n_blocks, TOKENS, PACK], BF16, name="hg", align_bytes=64)
        hcodes = keep.tile([P, n_blocks * TOKENS], U32, name="hcodes", align_bytes=64)
        hscales = keep.tile([P, n_blocks * TOKENS], U8, name="hscales", align_bytes=64)

        def load(u):
            kind, a, i, c = units[u]
            raw[u] = rawp.tile([P, PACK, UNIT], BF16, name="raw", tag="raw")
            if kind == "g":
                src = w_gating[i, c * K_PASS : (c + 1) * K_PASS, a * UNIT : (a + 1) * UNIT].rearrange(
                    "(p j) w -> p j w", j=PACK
                )
            else:
                src = w_linear[a * K_PASS : (a + 1) * K_PASS, :].rearrange("(t p) n -> p t n", p=P)
            nc.sync.dma_start(out=raw[u][:], in_=src)

        def regroup(u, lo, hi, cut):
            if u not in grp:
                grp[u] = grpp.tile([P, UNIT, PACK], BF16, name="grp", tag="grp", align_bytes=64)
            dst = grp[u][:, lo:cut, :].rearrange("p (c i) t -> p c t i", i=4)
            src = raw[u][:, :, lo:cut].rearrange("p t (c i) -> p c t i", i=4)
            nc.vector.tensor_copy(out=dst, in_=src)
            top = hi - GROUPS * GROUP if u in HELPED else hi
            dst = grp[u][:, cut:top, :].rearrange("p (c i) t -> p c t i", i=4)
            src = raw[u][:, :, cut:top].rearrange("p t (c i) -> p c t i", i=4)
            nc.scalar.copy(out=dst, in_=src)
            for k in range((hi - top) // GROUP):
                cols = slice(top + k * GROUP, top + (k + 1) * GROUP)
                nc.scalar.copy(out=grp[u][:, cols, :], in_=woven[(u, k)][:])

        def weave(u):
            top = UNIT - GROUPS * GROUP
            for k in range(GROUPS):
                cols = slice(top + k * GROUP, top + (k + 1) * GROUP)
                bank = psum.tile([P, GROUP, PACK], BF16, name="woven", tag="ps%d" % (4 + 2 * (u % 2) + k))
                woven[(u, k)] = bank
                words = bank[:].rearrange("p c t -> p (c t)").bitcast(F32).rearrange("p (c h) -> p c h", h=2)
                for h in range(2):
                    nc.tensor.matmul(
                        out=words[:, :, h], lhsT=ident_bf[:], rhs=raw[u][:, 2 * h + 1, cols], start=True, stop=True
                    )
                for h in range(2):
                    nc.tensor.matmul(
                        out=bank[:, :, 2 * h], lhsT=ident_bf[:], rhs=raw[u][:, 2 * h, cols], start=True, stop=True
                    )

        def quantise(u, lo, hi):
            if u not in codes:
                codes[u] = codp.tile([P, UNIT], U32, name="codes", tag="codes", align_bytes=64)
                scales[u] = codp.tile([P, UNIT], U8, name="scales", tag="scales", align_bytes=64)
            nc.vector.quantize_mx(
                out=codes[u][:, lo:hi].bitcast(FP8X4),
                scales=scales[u][:, lo:hi],
                in_=grp[u][:, lo:hi, :].rearrange("p w j -> p (w j)"),
            )

        def stage1(e):
            g, a = e // 2, e % 2
            r, off = g // 2, (g % 2) * K_PASS
            q = pair_of(e)
            gate_ps[e] = psum.tile([P, PACK, P], F32, name="gate_ps", tag="ps%d" % (2 * q))
            lin_ps[e] = psum.tile([P, PACK, P], F32, name="lin_ps", tag="ps%d" % (2 * q + 1))
            for i, bank in ((0, gate_ps[e]), (1, lin_ps[e])):
                for t in range(PACK):
                    for c in range(2):
                        u = 4 * r + 2 * i + c
                        cols = slice(off + t * P, off + (t + 1) * P)
                        toks = slice(c * TOKENS + a * P, c * TOKENS + (a + 1) * P)
                        nc.tensor.matmul_mx(
                            out=bank[:, t, :],
                            lhsT=codes[u][:, cols].bitcast(FP8X4),
                            lhsT_scale=scales[u][:, cols],
                            rhs=xcodes[:, toks].bitcast(FP8X4),
                            rhs_scale=xscales[:, toks],
                            start=(c == 0),
                            stop=(c == 1),
                        )

        def gelu(e):
            gel[e] = gelp.tile([P, P, PACK], F32, name="gel", tag="gel")
            nc.scalar.activation(out=gel[e][:], in_=gate_ps[e][:].rearrange("p t k -> p k t"), func=GELU)

        def gated(e):
            g, a = e // 2, e % 2
            nc.vector.tensor_tensor(
                out=hg[:, g, a * P : (a + 1) * P, :],
                in0=gel[e][:],
                in1=lin_ps[e][:].rearrange("p t k -> p k t"),
                op=MULT,
            )

        def quantise_h(g):
            cols = slice(g * TOKENS, (g + 1) * TOKENS)
            nc.vector.quantize_mx(
                out=hcodes[:, cols].bitcast(FP8X4),
                scales=hscales[:, cols],
                in_=hg[:, g, :, :].rearrange("p k t -> p (k t)"),
            )

        def stage2(g, halves):
            u = n_gate_units + g
            for nh in halves:
                for a in range(2):
                    if (a, nh) not in out_ps:
                        out_ps[(a, nh)] = psum.tile([P, 512], F32, name="out_ps", tag="ps%d" % (4 + 2 * a + nh))
                    toks = slice(g * TOKENS + a * P, g * TOKENS + (a + 1) * P)
                    cols = slice(nh * 512, (nh + 1) * 512)
                    nc.tensor.matmul_mx(
                        out=out_ps[(a, nh)][:],
                        lhsT=hcodes[:, toks].bitcast(FP8X4),
                        lhsT_scale=hscales[:, toks],
                        rhs=codes[u][:, cols].bitcast(FP8X4),
                        rhs_scale=scales[u][:, cols],
                        start=(g == 0),
                        stop=(g == n_blocks - 1),
                    )

        def store(a, nh, on_vector):
            res = ostp.tile([P, 512], F32, name="res", tag="res")
            if on_vector:
                nc.vector.tensor_copy(out=res[:], in_=out_ps[(a, nh)][:])
            else:
                nc.scalar.copy(out=res[:], in_=out_ps[(a, nh)][:])
            nc.sync.dma_start(out=out[a, :, nh * 512 : (nh + 1) * 512], in_=res[:])

        def cut_of(u):
            if u in HELPED:
                return CUT_HELPED
            return CUT_BUSY if gelu_slot[0] <= u - 1 <= mul_slot[-1] else CUT_PLAIN

        nc.vector.memset(warm_in[:], 0.0)
        nc.scalar.activation(out=warm_out[:], in_=warm_in[:], func=GELU)
        make_identity(nc, ident[:])
        make_identity(nc, ident_bf[:])
        for u in range(RAW_BUFS):
            load(u)
            if u == X_AFTER:
                nc.sync.dma_start(
                    out=x_sb[:].rearrange("p (a k) -> p a k", a=2), in_=x.rearrange("a p k -> p a k")
                )
        xw = x_sb[:].bitcast(F32).rearrange("p (a c w u) -> p a c u w", a=2, c=2, w=P, u=2)
        xgw = xg[:].bitcast(F32).rearrange("p (c k u) -> p c k u", c=2, k=TOKENS, u=2)
        xt = {}
        for c in range(2):
            xt[c] = psum.tile([P, 2, TOKENS], F32, name="xt", tag="ps%d" % c)
            for u in range(2):
                for a in range(2):
                    nc.tensor.transpose(xt[c][:, u, a * P : (a + 1) * P], xw[:, a, c, u, :], ident[:])
        regroup(0, 0, UNIT, cut_of(0))
        load(RAW_BUFS)

        last = n_units - 1
        for s in range(n_units):
            nxt = s + 1
            if nxt < last:
                regroup(nxt, 0, UNIT, cut_of(nxt))
            elif nxt == last:
                regroup(nxt, 0, UNIT // 2, cut_of(nxt) // 2)
                regroup(nxt, UNIT // 2, UNIT, UNIT // 2 + cut_of(nxt) // 2)
            if nxt + RAW_BUFS < n_units:
                load(nxt + RAW_BUFS)
            if s < last:
                quantise(s, 0, UNIT)
            else:
                quantise(s, 0, UNIT // 2)
            if s == X_SLOT:
                nc.vector.tensor_copy(out=xgw[:, 0], in_=xt[0][:].rearrange("p u k -> p k u"))
                nc.scalar.copy(out=xgw[:, 1], in_=xt[1][:].rearrange("p u k -> p k u"))
            if s == X_SLOT + 1:
                nc.vector.quantize_mx(out=xcodes[:].bitcast(FP8X4), scales=xscales[:], in_=xg[:])
            for e in range(n_epi):
                if gelu_slot[e] == s:
                    gelu(e)
            for e in range(n_epi):
                if mul_slot[e] == s:
                    gated(e)
            for g in range(n_blocks):
                if qh_slot[g] == s:
                    quantise_h(g)
            if s + 2 in HELPED:
                weave(s + 2)
            for e in range(n_epi):
                if mm1_slot[e] == s:
                    stage1(e)
            for g in range(n_blocks):
                if mm2_slot[g] == s:
                    if g < n_blocks - 1:
                        stage2(g, (0, 1))
                    else:
                        stage2(g, (0,))

        quantise(last, UNIT // 2, UNIT)
        stage2(n_blocks - 1, (1,))
        store(0, 0, False)
        store(1, 0, False)
        store(0, 1, True)
        store(1, 1, False)
